import numpy as np
import ml_dtypes


def mxq(x, axis, fmt="e4m3"):
    dtype, down = {"e4m3": (ml_dtypes.float8_e4m3fn, 7), "e5m2": (ml_dtypes.float8_e5m2, 14)}[fmt]
    v = np.moveaxis(np.asarray(x, np.float32).astype(ml_dtypes.bfloat16).astype(np.float64), axis, -1)
    blocks = v.reshape(v.shape[:-1] + (-1, 32))
    amax = np.abs(blocks).max(-1, keepdims=True)
    byte = np.maximum(np.where(amax > 0, np.frexp(amax)[1] - 1 + 127, 0) - down, 1)
    scale = np.exp2(byte - 127.0)
    codes = (blocks / scale).astype(np.float32).astype(dtype).astype(np.float64)
    return np.moveaxis((codes * scale).reshape(v.shape), -1, axis)


WIDE = False


def mx_kscale(k):
    if not WIDE:
        return np.ones(k)
    levels = np.array([20, -20, 10, -10, 0])
    a = np.random.permutation(np.resize(levels, k // 512 * 4)).reshape(k // 512, 4)
    idx = np.arange(k)
    return np.exp2(a[idx // 512, idx % 128 // 32])


BF16 = ml_dtypes.bfloat16


def bf(x):
    return np.asarray(x, np.float32).astype(BF16)


def f64(x):
    return np.asarray(x).astype(np.float64)


B, S, D_IN, D_OUT = 4, 2048, 512, 512
T = B * S


def setup_inputs():
    s = mx_kscale(T).reshape(B, S, 1)
    x = np.random.standard_normal((B, S, D_IN)) * s
    weight = np.random.standard_normal((D_OUT, D_IN)) * 0.04
    g = np.random.standard_normal((B, S, D_OUT)) * np.exp2(np.random.randint(-12, 1, (B, S, 1))) * 0.25 / s
    return {"x": bf(x), "weight": bf(weight), "grad_out": bf(g)}


def reference(x, weight, grad_out):
    x2 = f64(x).reshape(T, D_IN)
    g2 = f64(grad_out).reshape(T, D_OUT)
    gq = mxq(g2, 0, "e5m2")
    xq = mxq(x2, 0, "e4m3")
    return gq.T @ xq

@@ -1,0 +1,101 @@
+from contextlib import ExitStack
+
+import concourse.mybir as mybir
+
+BF16 = mybir.dt.bfloat16
+F32 = mybir.dt.float32
+U32 = mybir.dt.uint32
+U8 = mybir.dt.uint8
+E4M3X4 = mybir.dt.float8_e4m3fn_x4
+E5M2X4 = mybir.dt.float8_e5m2_x4
+
+P = 128
+PACK = 4
+K_PASS = P * PACK
+T = 8192
+D_IN = 512
+D_OUT = 512
+PASSES = T // K_PASS
+M_TILES = D_OUT // P
+
+FLOPS = 2 * T * D_IN * D_OUT
+BYTES = 2 * T * (D_IN + D_OUT) + 4 * D_IN * D_OUT
+
+
+def tile_fp8purelinear_kernel(tc, x, weight, grad_out, out):
+    nc = tc.nc
+    x2 = x.flatten_outer_dims()
+    g2 = grad_out.flatten_outer_dims()
+
+    with ExitStack() as ctx:
+        raw = ctx.enter_context(tc.tile_pool(name="raw", bufs=PASSES))
+        work = ctx.enter_context(tc.tile_pool(name="work", bufs=3))
+        res_pool = ctx.enter_context(tc.tile_pool(name="res", bufs=M_TILES))
+        psum = ctx.enter_context(tc.psum_pool(name="acc", bufs=1))
+        ctx.enter_context(tc.manual_schedule())
+
+        acc = [psum.tile([P, D_IN], F32, name="acc%d" % m) for m in range(M_TILES)]
+
+        def load(src, c, tag):
+            t = raw.tile([P, PACK, 512], BF16, name="%s%d" % (tag, c), tag=tag)
+            rows = src[c * K_PASS : (c + 1) * K_PASS, :]
+            nc.sync.dma_start(out=t[:], in_=rows.rearrange("(p j) w -> p j w", j=PACK))
+            return t
+
+        def regroup(engine_copy, t, tag, c):
+            grouped = work.tile([P, 512, PACK], BF16, name="%s%d" % (tag, c), tag=tag, align_bytes=64)
+            engine_copy(
+                out=grouped[:].rearrange("p (c i) t -> p c t i", i=4),
+                in_=t[:].rearrange("p t (c i) -> p c t i", i=4),
+            )
+            return grouped
+
+        def quantise(grouped, fmt, tag, c):
+            codes = work.tile([P, 512], U32, name="%sc%d" % (tag, c), tag=tag + "c", align_bytes=64)
+            scales = work.tile([P, 512], U8, name="%ss%d" % (tag, c), tag=tag + "s", align_bytes=64)
+            nc.vector.quantize_mx(
+                out=codes[:].bitcast(fmt),
+                scales=scales[:],
+                in_=grouped[:].rearrange("p w j -> p (w j)"),
+            )
+            return codes, scales
+
+        def multiply(c, gq, xq):
+            for m in range(M_TILES):
+                cols = slice(m * P, (m + 1) * P)
+                nc.tensor.matmul_mx(
+                    out=acc[m][:],
+                    lhsT=gq[0][:, cols].bitcast(E5M2X4),
+                    lhsT_scale=gq[1][:, cols],
+                    rhs=xq[0][:].bitcast(E4M3X4),
+                    rhs_scale=xq[1][:],
+                    start=(c == 0),
+                    stop=(c == PASSES - 1),
+                )
+
+        x_raw = []
+        g_raw = []
+        for c in range(PASSES):
+            x_raw.append(load(x2, c, "xr"))
+            g_raw.append(load(g2, c, "gr"))
+
+        x_grouped = [None] * PASSES
+        g_q = [None] * PASSES
+        for c in range(PASSES + 1):
+            if c < PASSES:
+                x_grouped[c] = regroup(nc.scalar.copy, x_raw[c], "xg", c)
+                g_grouped = regroup(nc.vector.tensor_copy, g_raw[c], "gg", c)
+            if c > 0:
+                x_q = quantise(x_grouped[c - 1], E4M3X4, "x", c - 1)
+            if c < PASSES:
+                g_q[c] = quantise(g_grouped, E5M2X4, "g", c)
+            if c > 0:
+                multiply(c - 1, g_q[c - 1], x_q)
+
+        for m in range(M_TILES):
+            res = res_pool.tile([P, D_IN], F32, name="res%d" % m, tag="res")
+            if m % 2 == 0:
+                nc.vector.tensor_copy(out=res[:], in_=acc[m][:])
+            else:
+                nc.scalar.copy(out=res[:], in_=acc[m][:])
+            nc.sync.dma_start(out=out[m * P : (m + 1) * P, :], in_=res[:])

@@ -13,13 +13,13 @@ P = 128
 PACK = 4
 K_PASS = P * PACK
 T = 8192
-D_IN = 512
-D_OUT = 512
+D = 512
 PASSES = T // K_PASS
-M_TILES = D_OUT // P
+M_TILES = D // P
+V_COLS = 248
 
-FLOPS = 2 * T * D_IN * D_OUT
-BYTES = 2 * T * (D_IN + D_OUT) + 4 * D_IN * D_OUT
+FLOPS = 2 * T * D * D
+BYTES = 2 * T * (D + D) + 4 * D * D
 
 
 def tile_fp8purelinear_kernel(tc, x, weight, grad_out, out):
@@ -28,74 +28,81 @@ def tile_fp8purelinear_kernel(tc, x, weight, grad_out, out):
     g2 = grad_out.flatten_outer_dims()
 
     with ExitStack() as ctx:
-        raw = ctx.enter_context(tc.tile_pool(name="raw", bufs=PASSES))
-        work = ctx.enter_context(tc.tile_pool(name="work", bufs=3))
+        raw_pool = ctx.enter_context(tc.tile_pool(name="raw", bufs=2 * PASSES))
+        grp_pool = ctx.enter_context(tc.tile_pool(name="grp", bufs=4))
+        q_pool = ctx.enter_context(tc.tile_pool(name="q", bufs=3))
         res_pool = ctx.enter_context(tc.tile_pool(name="res", bufs=M_TILES))
         psum = ctx.enter_context(tc.psum_pool(name="acc", bufs=1))
         ctx.enter_context(tc.manual_schedule())
 
-        acc = [psum.tile([P, D_IN], F32, name="acc%d" % m) for m in range(M_TILES)]
+        acc = [psum.tile([P, D], F32, name="acc%d" % m) for m in range(M_TILES)]
 
-        def load(src, c, tag):
-            t = raw.tile([P, PACK, 512], BF16, name="%s%d" % (tag, c), tag=tag)
-            rows = src[c * K_PASS : (c + 1) * K_PASS, :]
+        chunks = [(src, c) for c in range(PASSES) for src in ("x", "g")]
+        raw = []
+        for src, c in chunks:
+            t = raw_pool.tile([P, PACK, D], BF16, name="raw_%s%d" % (src, c), tag="raw")
+            rows = (x2 if src == "x" else g2)[c * K_PASS : (c + 1) * K_PASS, :]
             nc.sync.dma_start(out=t[:], in_=rows.rearrange("(p j) w -> p j w", j=PACK))
-            return t
+            raw.append(t)
 
-        def regroup(engine_copy, t, tag, c):
-            grouped = work.tile([P, 512, PACK], BF16, name="%s%d" % (tag, c), tag=tag, align_bytes=64)
+        def regroup(engine_copy, grouped, t, lo, hi):
             engine_copy(
-                out=grouped[:].rearrange("p (c i) t -> p c t i", i=4),
-                in_=t[:].rearrange("p t (c i) -> p c t i", i=4),
+                out=grouped[:, lo:hi, :].rearrange("p (c i) t -> p c t i", i=4),
+                in_=t[:, :, lo:hi].rearrange("p t (c i) -> p c t i", i=4),
             )
-            return grouped
 
-        def quantise(grouped, fmt, tag, c):
-            codes = work.tile([P, 512], U32, name="%sc%d" % (tag, c), tag=tag + "c", align_bytes=64)
-            scales = work.tile([P, 512], U8, name="%ss%d" % (tag, c), tag=tag + "s", align_bytes=64)
+        def quantise(grouped, codes, scales, fmt, lo, hi):
             nc.vector.quantize_mx(
-                out=codes[:].bitcast(fmt),
-                scales=scales[:],
-                in_=grouped[:].rearrange("p w j -> p (w j)"),
+                out=codes[:, lo:hi].bitcast(fmt),
+                scales=scales[:, lo:hi],
+                in_=grouped[:, lo:hi, :].rearrange("p w j -> p (w j)"),
             )
-            return codes, scales
 
-        def multiply(c, gq, xq):
-            for m in range(M_TILES):
-                cols = slice(m * P, (m + 1) * P)
-                nc.tensor.matmul_mx(
-                    out=acc[m][:],
-                    lhsT=gq[0][:, cols].bitcast(E5M2X4),
-                    lhsT_scale=gq[1][:, cols],
-                    rhs=xq[0][:].bitcast(E4M3X4),
-                    rhs_scale=xq[1][:],
-                    start=(c == 0),
-                    stop=(c == PASSES - 1),
-                )
+        def multiply(c, m, gq, xq):
+            cols = slice(m * P, (m + 1) * P)
+            nc.tensor.matmul_mx(
+                out=acc[m][:],
+                lhsT=gq[0][:, cols].bitcast(E5M2X4),
+                lhsT_scale=gq[1][:, cols],
+                rhs=xq[0][:].bitcast(E4M3X4),
+                rhs_scale=xq[1][:],
+                start=(c == 0),
+                stop=(c == PASSES - 1),
+            )
 
-        x_raw = []
-        g_raw = []
-        for c in range(PASSES):
-            x_raw.append(load(x2, c, "xr"))
-            g_raw.append(load(g2, c, "gr"))
-
-        x_grouped = [None] * PASSES
-        g_q = [None] * PASSES
-        for c in range(PASSES + 1):
-            if c < PASSES:
-                x_grouped[c] = regroup(nc.scalar.copy, x_raw[c], "xg", c)
-                g_grouped = regroup(nc.vector.tensor_copy, g_raw[c], "gg", c)
-            if c > 0:
-                x_q = quantise(x_grouped[c - 1], E4M3X4, "x", c - 1)
-            if c < PASSES:
-                g_q[c] = quantise(g_grouped, E5M2X4, "g", c)
-            if c > 0:
-                multiply(c - 1, g_q[c - 1], x_q)
-
-        for m in range(M_TILES):
-            res = res_pool.tile([P, D_IN], F32, name="res%d" % m, tag="res")
-            if m % 2 == 0:
-                nc.vector.tensor_copy(out=res[:], in_=acc[m][:])
+        n = len(chunks)
+        grouped = [None] * n
+        quantised = [None] * n
+        for i in range(n):
+            src, c = chunks[i]
+            grouped[i] = grp_pool.tile([P, D, PACK], BF16, name="grp%d" % i, tag="grp", align_bytes=64)
+            quantised[i] = (
+                q_pool.tile([P, D], U32, name="codes%d" % i, tag=src + "c", align_bytes=64),
+                q_pool.tile([P, D], U8, name="scales%d" % i, tag=src + "s", align_bytes=64),
+            )
+            if i < n - 1:
+                regroup(nc.vector.tensor_copy, grouped[i], raw[i], 0, V_COLS)
+                regroup(nc.scalar.copy, grouped[i], raw[i], V_COLS, D)
             else:
+                regroup(nc.vector.tensor_copy, grouped[i], raw[i], 0, 2 * P)
+                regroup(nc.scalar.copy, grouped[i], raw[i], 2 * P, 3 * P)
+                regroup(nc.scalar.copy, grouped[i], raw[i], 3 * P, 4 * P)
+            if i > 0:
+                prev_src, prev_c = chunks[i - 1]
+                fmt = E4M3X4 if prev_src == "x" else E5M2X4
+                quantise(grouped[i - 1], quantised[i - 1][0], quantised[i - 1][1], fmt, 0, D)
+                if prev_src == "g":
+                    for m in range(M_TILES):
+                        multiply(prev_c, m, quantised[i - 1], quantised[i - 2])
+
+        last = n - 1
+        for m in range(M_TILES):
+            quantise(grouped[last], quantised[last][0], quantised[last][1], E5M2X4, m * P, (m + 1) * P)
+            multiply(PASSES - 1, m, quantised[last], quantised[last - 1])
+        for m in range(M_TILES):
+            res = res_pool.tile([P, D], F32, name="res%d" % m, tag="res")
+            if m % 2 == 0:
                 nc.scalar.copy(out=res[:], in_=acc[m][:])
+            else:
+                nc.vector.tensor_copy(out=res[:], in_=acc[m][:])
             nc.sync.dma_start(out=out[m * P : (m + 1) * P, :], in_=res[:])

@@ -1,6 +1,7 @@
 from contextlib import ExitStack
 
 import concourse.mybir as mybir
+from concourse.masks import make_identity
 
 BF16 = mybir.dt.bfloat16
 F32 = mybir.dt.float32
@@ -17,6 +18,8 @@ D = 512
 PASSES = T // K_PASS
 M_TILES = D // P
 V_COLS = 248
+V_COLS_PE = 200
+PE_LO = D - P
 
 FLOPS = 2 * T * D * D
 BYTES = 2 * T * (D + D) + 4 * D * D
@@ -32,8 +35,13 @@ def tile_fp8purelinear_kernel(tc, x, weight, grad_out, out):
         grp_pool = ctx.enter_context(tc.tile_pool(name="grp", bufs=4))
         q_pool = ctx.enter_context(tc.tile_pool(name="q", bufs=3))
         res_pool = ctx.enter_context(tc.tile_pool(name="res", bufs=M_TILES))
+        const = ctx.enter_context(tc.tile_pool(name="const", bufs=1))
         psum = ctx.enter_context(tc.psum_pool(name="acc", bufs=1))
+        mv_pool = ctx.enter_context(tc.psum_pool(name="mv", bufs=4))
         ctx.enter_context(tc.manual_schedule())
+
+        ident = const.tile([P, P], BF16, name="ident")
+        make_identity(nc, ident[:])
 
         acc = [psum.tile([P, D], F32, name="acc%d" % m) for m in range(M_TILES)]
 
@@ -50,6 +58,17 @@ def tile_fp8purelinear_kernel(tc, x, weight, grad_out, out):
                 out=grouped[:, lo:hi, :].rearrange("p (c i) t -> p c t i", i=4),
                 in_=t[:, :, lo:hi].rearrange("p t (c i) -> p c t i", i=4),
             )
+
+        def regroup_on_tensor(i, t):
+            mv = mv_pool.tile([P, P, PACK], BF16, name="mv%d" % i, tag="mv")
+            nc.tensor.matmul(
+                out=mv[:].rearrange("p w t -> p t w"),
+                lhsT=ident[:],
+                rhs=t[:, :, PE_LO:D],
+                start=True,
+                stop=True,
+            )
+            return mv
 
         def quantise(grouped, codes, scales, fmt, lo, hi):
             nc.vector.quantize_mx(
@@ -80,13 +99,21 @@ def tile_fp8purelinear_kernel(tc, x, weight, grad_out, out):
                 q_pool.tile([P, D], U32, name="codes%d" % i, tag=src + "c", align_bytes=64),
                 q_pool.tile([P, D], U8, name="scales%d" % i, tag=src + "s", align_bytes=64),
             )
-            if i < n - 1:
+            helped = i % 4 != 0
+            if helped:
+                mv = regroup_on_tensor(i, raw[i])
+            if not helped:
                 regroup(nc.vector.tensor_copy, grouped[i], raw[i], 0, V_COLS)
                 regroup(nc.scalar.copy, grouped[i], raw[i], V_COLS, D)
+            elif i < n - 1:
+                regroup(nc.vector.tensor_copy, grouped[i], raw[i], 0, V_COLS_PE)
+                regroup(nc.scalar.copy, grouped[i], raw[i], V_COLS_PE, PE_LO)
             else:
-                regroup(nc.vector.tensor_copy, grouped[i], raw[i], 0, 2 * P)
+                regroup(nc.vector.tensor_copy, grouped[i], raw[i], 0, P)
+                regroup(nc.scalar.copy, grouped[i], raw[i], P, 2 * P)
                 regroup(nc.scalar.copy, grouped[i], raw[i], 2 * P, 3 * P)
-                regroup(nc.scalar.copy, grouped[i], raw[i], 3 * P, 4 * P)
+            if helped:
+                nc.scalar.copy(out=grouped[i][:, PE_LO:D, :], in_=mv[:])
             if i > 0:
                 prev_src, prev_c = chunks[i - 1]
                 fmt = E4M3X4 if prev_src == "x" else E5M2X4

@@ -92,6 +92,7 @@ def tile_fp8purelinear_kernel(tc, x, weight, grad_out, out):
         n = len(chunks)
         grouped = [None] * n
         quantised = [None] * n
+        moved = [None] * n
         for i in range(n):
             src, c = chunks[i]
             grouped[i] = grp_pool.tile([P, D, PACK], BF16, name="grp%d" % i, tag="grp", align_bytes=64)
@@ -100,8 +101,6 @@ def tile_fp8purelinear_kernel(tc, x, weight, grad_out, out):
                 q_pool.tile([P, D], U8, name="scales%d" % i, tag=src + "s", align_bytes=64),
             )
             helped = i % 4 != 0
-            if helped:
-                mv = regroup_on_tensor(i, raw[i])
             if not helped:
                 regroup(nc.vector.tensor_copy, grouped[i], raw[i], 0, V_COLS)
                 regroup(nc.scalar.copy, grouped[i], raw[i], V_COLS, D)
@@ -113,7 +112,9 @@ def tile_fp8purelinear_kernel(tc, x, weight, grad_out, out):
                 regroup(nc.scalar.copy, grouped[i], raw[i], P, 2 * P)
                 regroup(nc.scalar.copy, grouped[i], raw[i], 2 * P, 3 * P)
             if helped:
-                nc.scalar.copy(out=grouped[i][:, PE_LO:D, :], in_=mv[:])
+                nc.scalar.copy(out=grouped[i][:, PE_LO:D, :], in_=moved[i][:])
+            if i + 1 < n and (i + 1) % 4 != 0:
+                moved[i + 1] = regroup_on_tensor(i + 1, raw[i + 1])
             if i > 0:
                 prev_src, prev_c = chunks[i - 1]
                 fmt = E4M3X4 if prev_src == "x" else E5M2X4

@@ -1,7 +1,6 @@
 from contextlib import ExitStack
 
 import concourse.mybir as mybir
-from concourse.masks import make_identity
 
 BF16 = mybir.dt.bfloat16
 F32 = mybir.dt.float32
@@ -18,8 +17,6 @@ D = 512
 PASSES = T // K_PASS
 M_TILES = D // P
 V_COLS = 248
-V_COLS_PE = 200
-PE_LO = D - P
 
 FLOPS = 2 * T * D * D
 BYTES = 2 * T * (D + D) + 4 * D * D
@@ -35,13 +32,8 @@ def tile_fp8purelinear_kernel(tc, x, weight, grad_out, out):
         grp_pool = ctx.enter_context(tc.tile_pool(name="grp", bufs=4))
         q_pool = ctx.enter_context(tc.tile_pool(name="q", bufs=3))
         res_pool = ctx.enter_context(tc.tile_pool(name="res", bufs=M_TILES))
-        const = ctx.enter_context(tc.tile_pool(name="const", bufs=1))
         psum = ctx.enter_context(tc.psum_pool(name="acc", bufs=1))
-        mv_pool = ctx.enter_context(tc.psum_pool(name="mv", bufs=4))
         ctx.enter_context(tc.manual_schedule())
-
-        ident = const.tile([P, P], BF16, name="ident")
-        make_identity(nc, ident[:])
 
         acc = [psum.tile([P, D], F32, name="acc%d" % m) for m in range(M_TILES)]
 
@@ -58,17 +50,6 @@ def tile_fp8purelinear_kernel(tc, x, weight, grad_out, out):
                 out=grouped[:, lo:hi, :].rearrange("p (c i) t -> p c t i", i=4),
                 in_=t[:, :, lo:hi].rearrange("p t (c i) -> p c t i", i=4),
             )
-
-        def regroup_on_tensor(i, t):
-            mv = mv_pool.tile([P, P, PACK], BF16, name="mv%d" % i, tag="mv")
-            nc.tensor.matmul(
-                out=mv[:].rearrange("p w t -> p t w"),
-                lhsT=ident[:],
-                rhs=t[:, :, PE_LO:D],
-                start=True,
-                stop=True,
-            )
-            return mv
 
         def quantise(grouped, codes, scales, fmt, lo, hi):
             nc.vector.quantize_mx(
@@ -92,7 +73,6 @@ def tile_fp8purelinear_kernel(tc, x, weight, grad_out, out):
         n = len(chunks)
         grouped = [None] * n
         quantised = [None] * n
-        moved = [None] * n
         for i in range(n):
             src, c = chunks[i]
             grouped[i] = grp_pool.tile([P, D, PACK], BF16, name="grp%d" % i, tag="grp", align_bytes=64)
@@ -100,21 +80,14 @@ def tile_fp8purelinear_kernel(tc, x, weight, grad_out, out):
                 q_pool.tile([P, D], U32, name="codes%d" % i, tag=src + "c", align_bytes=64),
                 q_pool.tile([P, D], U8, name="scales%d" % i, tag=src + "s", align_bytes=64),
             )
-            helped = i % 4 != 0
-            if not helped:
+            if i < n - 1:
                 regroup(nc.vector.tensor_copy, grouped[i], raw[i], 0, V_COLS)
                 regroup(nc.scalar.copy, grouped[i], raw[i], V_COLS, D)
-            elif i < n - 1:
-                regroup(nc.vector.tensor_copy, grouped[i], raw[i], 0, V_COLS_PE)
-                regroup(nc.scalar.copy, grouped[i], raw[i], V_COLS_PE, PE_LO)
             else:
                 regroup(nc.vector.tensor_copy, grouped[i], raw[i], 0, P)
                 regroup(nc.scalar.copy, grouped[i], raw[i], P, 2 * P)
                 regroup(nc.scalar.copy, grouped[i], raw[i], 2 * P, 3 * P)
-            if helped:
-                nc.scalar.copy(out=grouped[i][:, PE_LO:D, :], in_=moved[i][:])
-            if i + 1 < n and (i + 1) % 4 != 0:
-                moved[i + 1] = regroup_on_tensor(i + 1, raw[i + 1])
+                regroup(nc.scalar.copy, grouped[i], raw[i], 3 * P, 4 * P)
             if i > 0:
                 prev_src, prev_c = chunks[i - 1]
                 fmt = E4M3X4 if prev_src == "x" else E5M2X4

from contextlib import ExitStack

import concourse.mybir as mybir

BF16 = mybir.dt.bfloat16
F32 = mybir.dt.float32
U32 = mybir.dt.uint32
U8 = mybir.dt.uint8
E4M3X4 = mybir.dt.float8_e4m3fn_x4
E5M2X4 = mybir.dt.float8_e5m2_x4

P = 128
PACK = 4
K_PASS = P * PACK
T = 8192
D = 512
PASSES = T // K_PASS
M_TILES = D // P
V_COLS = 248

FLOPS = 2 * T * D * D
BYTES = 2 * T * (D + D) + 4 * D * D


def tile_fp8purelinear_kernel(tc, x, weight, grad_out, out):
    nc = tc.nc
    x2 = x.flatten_outer_dims()
    g2 = grad_out.flatten_outer_dims()

    with ExitStack() as ctx:
        raw_pool = ctx.enter_context(tc.tile_pool(name="raw", bufs=2 * PASSES))
        grp_pool = ctx.enter_context(tc.tile_pool(name="grp", bufs=4))
        q_pool = ctx.enter_context(tc.tile_pool(name="q", bufs=3))
        res_pool = ctx.enter_context(tc.tile_pool(name="res", bufs=M_TILES))
        psum = ctx.enter_context(tc.psum_pool(name="acc", bufs=1))
        ctx.enter_context(tc.manual_schedule())

        acc = [psum.tile([P, D], F32, name="acc%d" % m) for m in range(M_TILES)]

        chunks = [(src, c) for c in range(PASSES) for src in ("x", "g")]
        raw = []
        for src, c in chunks:
            t = raw_pool.tile([P, PACK, D], BF16, name="raw_%s%d" % (src, c), tag="raw")
            rows = (x2 if src == "x" else g2)[c * K_PASS : (c + 1) * K_PASS, :]
            nc.sync.dma_start(out=t[:], in_=rows.rearrange("(p j) w -> p j w", j=PACK))
            raw.append(t)

        def regroup(engine_copy, grouped, t, lo, hi):
            engine_copy(
                out=grouped[:, lo:hi, :].rearrange("p (c i) t -> p c t i", i=4),
                in_=t[:, :, lo:hi].rearrange("p t (c i) -> p c t i", i=4),
            )

        def quantise(grouped, codes, scales, fmt, lo, hi):
            nc.vector.quantize_mx(
                out=codes[:, lo:hi].bitcast(fmt),
                scales=scales[:, lo:hi],
                in_=grouped[:, lo:hi, :].rearrange("p w j -> p (w j)"),
            )

        def multiply(c, m, gq, xq):
            cols = slice(m * P, (m + 1) * P)
            nc.tensor.matmul_mx(
                out=acc[m][:],
                lhsT=gq[0][:, cols].bitcast(E5M2X4),
                lhsT_scale=gq[1][:, cols],
                rhs=xq[0][:].bitcast(E4M3X4),
                rhs_scale=xq[1][:],
                start=(c == 0),
                stop=(c == PASSES - 1),
            )

        n = len(chunks)
        grouped = [None] * n
        quantised = [None] * n
        for i in range(n):
            src, c = chunks[i]
            grouped[i] = grp_pool.tile([P, D, PACK], BF16, name="grp%d" % i, tag="grp", align_bytes=64)
            quantised[i] = (
                q_pool.tile([P, D], U32, name="codes%d" % i, tag=src + "c", align_bytes=64),
                q_pool.tile([P, D], U8, name="scales%d" % i, tag=src + "s", align_bytes=64),
            )
            if i < n - 1:
                regroup(nc.vector.tensor_copy, grouped[i], raw[i], 0, V_COLS)
                regroup(nc.scalar.copy, grouped[i], raw[i], V_COLS, D)
            else:
                regroup(nc.vector.tensor_copy, grouped[i], raw[i], 0, P)
                regroup(nc.scalar.copy, grouped[i], raw[i], P, 2 * P)
                regroup(nc.scalar.copy, grouped[i], raw[i], 2 * P, 3 * P)
                regroup(nc.scalar.copy, grouped[i], raw[i], 3 * P, 4 * P)
            if i > 0:
                prev_src, prev_c = chunks[i - 1]
                fmt = E4M3X4 if prev_src == "x" else E5M2X4
                quantise(grouped[i - 1], quantised[i - 1][0], quantised[i - 1][1], fmt, 0, D)
                if prev_src == "g":
                    for m in range(M_TILES):
                        multiply(prev_c, m, quantised[i - 1], quantised[i - 2])

        last = n - 1
        for m in range(M_TILES):
            quantise(grouped[last], quantised[last][0], quantised[last][1], E5M2X4, m * P, (m + 1) * P)
            multiply(PASSES - 1, m, quantised[last], quantised[last - 1])
        for m in range(M_TILES):
            res = res_pool.tile([P, D], F32, name="res%d" % m, tag="res")
            if m % 2 == 0:
                nc.scalar.copy(out=res[:], in_=acc[m][:])
            else:
                nc.vector.tensor_copy(out=res[:], in_=acc[m][:])
            nc.sync.dma_start(out=out[m * P : (m + 1) * P, :], in_=res[:])
